import numpy as np
import ml_dtypes


def mxq(x, axis, fmt="e4m3"):
    dtype, down = {"e4m3": (ml_dtypes.float8_e4m3fn, 7), "e5m2": (ml_dtypes.float8_e5m2, 14)}[fmt]
    v = np.moveaxis(np.asarray(x, np.float32).astype(ml_dtypes.bfloat16).astype(np.float64), axis, -1)
    blocks = v.reshape(v.shape[:-1] + (-1, 32))
    amax = np.abs(blocks).max(-1, keepdims=True)
    byte = np.maximum(np.where(amax > 0, np.frexp(amax)[1] - 1 + 127, 0) - down, 1)
    scale = np.exp2(byte - 127.0)
    codes = (blocks / scale).astype(np.float32).astype(dtype).astype(np.float64)
    return np.moveaxis((codes * scale).reshape(v.shape), -1, axis)


WIDE = False


def mx_kscale(k):
    if not WIDE:
        return np.ones(k)
    levels = np.array([10, -10, 5, -5, 0])
    a = np.random.permutation(np.resize(levels, k // 512 * 4)).reshape(k // 512, 4)
    idx = np.arange(k)
    return np.exp2(a[idx // 512, idx % 128 // 32])


BF16 = ml_dtypes.bfloat16


def bf(x):
    return np.asarray(x, np.float32).astype(BF16)


def f64(x):
    return np.asarray(x).astype(np.float64)


BS, H, XDIM = 8192, 128, 256
IN = XDIM + 2 * H


def sigmoid(v):
    return 1.0 / (1.0 + np.exp(-v))


def setup_inputs():
    s = mx_kscale(IN)
    c = 1.0 / np.sqrt(IN)

    def draw_w():
        return bf(np.random.standard_normal((H, IN)) * c / s[None, :])

    def draw_b():
        return bf(np.random.standard_normal(H) * 0.3)

    return {
        "input_x": bf(np.random.standard_normal((BS, XDIM)) * s[:XDIM]),
        "previous_time": bf(np.random.standard_normal((BS, H)) * s[XDIM:XDIM + H]),
        "previous_layer": bf(np.random.standard_normal((BS, H)) * s[XDIM + H:]),
        "old_state": bf(np.random.standard_normal((BS, H)) * 0.5),
        "Wi": draw_w(), "bi": draw_b(),
        "Wf": draw_w(), "bf": draw_b(),
        "Wo": draw_w(), "bo": draw_b(),
        "Ws": draw_w(), "bs_state": draw_b(),
    }


def reference(input_x, previous_time, previous_layer, old_state, Wi, bi, Wf, bf, Wo, bo, Ws, bs_state):
    z = np.concatenate([f64(input_x), f64(previous_time), f64(previous_layer)], axis=1)
    W_all = np.concatenate([f64(Wi), f64(Wf), f64(Wo), f64(Ws)], axis=0)
    b_all = np.concatenate([f64(bi), f64(bf), f64(bo), f64(bs_state)], axis=0)
    proj = (mxq(z, 1, "e4m3") @ mxq(W_all, 1, "e4m3").T) + b_all
    gi, gf, go, gs = np.split(proj, 4, axis=1)
    input_gate = sigmoid(gi)
    forget_gate = sigmoid(gf)
    output_gate = sigmoid(go)
    new_state = forget_gate * f64(old_state) + input_gate * np.tanh(gs)
    new_hidden = output_gate * np.tanh(new_state)
    return new_hidden

@@ -1,0 +1,285 @@
+from contextlib import ExitStack
+
+import concourse.bass as bass
+import concourse.mybir as mybir
+import concourse.tile as tile
+from concourse.masks import make_identity
+
+F32 = mybir.dt.float32
+BF16 = mybir.dt.bfloat16
+U32 = mybir.dt.uint32
+U8 = mybir.dt.uint8
+FP8X4 = mybir.dt.float8_e4m3fn_x4
+ACT = mybir.ActivationFunctionType
+ALU = mybir.AluOpType
+
+P = 128
+BS, H, XDIM = 8192, 128, 256
+IN = XDIM + 2 * H
+NT = BS // P
+FLOPS = 2 * BS * IN * 4 * H
+
+CHUNKS = [4] * 16
+LOADS = [4, 4, 8, 16, 16, 16]
+CMODE = ["ACC"]
+
+
+def tile_rnn_unit_t_kernel(tc, input_x, previous_time, previous_layer, old_state,
+                                      Wi, bi, Wf, bf, Wo, bo, Ws, bs_state, out):
+    nc = tc.nc
+    n_chunks = len(CHUNKS)
+    starts = [sum(CHUNKS[:n]) for n in range(n_chunks)]
+    assert sum(CHUNKS) == NT and sum(LOADS) == NT
+
+    x_v = input_x.rearrange("(p t) k -> p (t k)", t=NT)
+    pt_v = previous_time.rearrange("(p t) k -> p t k", t=NT)
+    pl_v = previous_layer.rearrange("(p t) k -> p t k", t=NT)
+    old_v = old_state.rearrange("(p t) k -> p (t k)", t=NT)
+    out_v = out.rearrange("(p t) h -> p (t h)", t=NT)
+
+    with ExitStack() as ctx:
+        const = ctx.enter_context(tc.tile_pool(name="const", bufs=1))
+        res = ctx.enter_context(tc.tile_pool(name="res", bufs=1))
+        ring = ctx.enter_context(tc.tile_pool(name="ring", bufs=4))
+        psum = ctx.enter_context(tc.psum_pool(name="psum", bufs=8))
+        ctx.enter_context(tc.manual_schedule())
+
+        ident_f = const.tile([P, P], F32, name="ident_f")
+        make_identity(nc, ident_f[:])
+        ident_b = const.tile([P, P], BF16, name="ident_b")
+        make_identity(nc, ident_b[:])
+        brow = const.tile([P, P], BF16, name="brow")
+        nc.vector.memset(brow[:], 0.0)
+        warm = const.tile([P, 1], F32, name="warm")
+        nc.vector.memset(warm[:], 0.0)
+
+        group_of = {}
+        xg, zg, og = [], [], []
+
+        def load_group(g, a, b):
+            n = b - a
+            xt = res.tile([P, n * XDIM], BF16, name="x%d" % g)
+            nc.sync.dma_start(out=xt[:], in_=x_v[:, a * XDIM:b * XDIM])
+            zt = res.tile([P, n * 2 * H], BF16, name="ptl%d" % g)
+            zt4 = zt[:].rearrange("p (t s k) -> p t s k", s=2, k=H)
+            nc.sync.dma_start(out=zt4[:, :, 0, :], in_=pt_v[:, a:b, :])
+            nc.sync.dma_start(out=zt4[:, :, 1, :], in_=pl_v[:, a:b, :])
+            xg.append(xt)
+            zg.append(zt)
+            for t in range(a, b):
+                group_of[t] = (g, t - a)
+
+        def load_old(g, a, b):
+            ot = res.tile([P, (b - a) * H], BF16, name="old%d" % g)
+            nc.sync.dma_start(out=ot[:], in_=old_v[:, a * H:b * H])
+            og.append(ot)
+
+        bounds = [(sum(LOADS[:g]), sum(LOADS[:g + 1])) for g in range(len(LOADS))]
+        load_group(0, bounds[0][0], bounds[0][1])
+        w_dram = [Wi, Ws, Wf, Wo]
+        b_dram = [bi, bs_state, bf, bo]
+        w_sb = []
+        for g in range(4):
+            wt = const.tile([P, IN], BF16, name="w%d" % g)
+            nc.scalar.dma_start(out=wt[:], in_=w_dram[g])
+            w_sb.append(wt)
+        for g in range(4):
+            nc.scalar.dma_start(out=brow[g:g + 1, :], in_=b_dram[g].rearrange("(o h) -> o h", o=1))
+        nc.scalar.activation(out=warm[:], in_=warm[:], func=ACT.Sigmoid)
+        load_old(0, bounds[0][0], bounds[0][1])
+        for g in range(1, len(LOADS)):
+            load_group(g, bounds[g][0], bounds[g][1])
+            load_old(g, bounds[g][0], bounds[g][1])
+
+        w_codes, w_scales = [], []
+        for h in range(2):
+            wz = psum.tile([P, 2, 2 * P], F32, name="wz", tag="bank")
+            for gg in range(2):
+                words = w_sb[2 * h + gg][:].bitcast(F32)
+                for u in range(2):
+                    nc.tensor.transpose(out=wz[:, u, gg * P:(gg + 1) * P], in_=words[:, u * P:(u + 1) * P],
+                                        identity=ident_f[:])
+            wgrp = const.tile([P, 8 * P], BF16, name="wgrp%d" % h, align_bytes=64)
+            nc.scalar.copy(out=wgrp[:].bitcast(F32).rearrange("p (c u) -> p c u", u=2),
+                           in_=wz[:].rearrange("p u c -> p c u"))
+            wc = const.tile([P, 2 * P], U32, name="wc%d" % h, align_bytes=64)
+            ws = const.tile([P, 2 * P], U8, name="ws%d" % h, align_bytes=64)
+            w_codes.append((wgrp, wc, ws))
+        for h in range(2):
+            wgrp, wc, ws = w_codes[h]
+            nc.vector.quantize_mx(out=wc[:].bitcast(FP8X4), scales=ws[:], in_=wgrp[:])
+
+        bias = const.tile([P, 4], F32, name="bias")
+
+        st = {}
+
+        def ok(n):
+            return 0 <= n < n_chunks
+
+        def zt_stage(n):
+            if not ok(n):
+                return
+            w = CHUNKS[n]
+            banks = []
+            for h in range((w + 1) // 2):
+                wb = min(2, w - 2 * h)
+                zb = psum.tile([P, 2, wb * P], F32, name="zb", tag="bank")
+                for j in range(wb):
+                    g, r = group_of[starts[n] + 2 * h + j]
+                    for u, src in ((0, xg[g]), (1, zg[g])):
+                        nc.tensor.transpose(out=zb[:, u, j * P:(j + 1) * P],
+                                            in_=src[:].bitcast(F32)[:, r * P:(r + 1) * P],
+                                            identity=ident_f[:])
+                banks.append((zb, wb))
+            st["zb", n] = banks
+            grp = ring.tile([P, w * 4 * P], BF16, name="grp", tag="grp%d" % w, align_bytes=64)
+            st["grp", n] = grp
+
+        def zc_stage(n):
+            if not ok(n):
+                return
+            gw = st["grp", n][:].bitcast(F32)
+            c0 = 0
+            for zb, wb in st["zb", n]:
+                nc.vector.tensor_copy(out=gw[:, 2 * c0:2 * (c0 + wb * P)].rearrange("p (c u) -> p c u", u=2),
+                                      in_=zb[:].rearrange("p u c -> p c u"))
+                c0 += wb * P
+
+        def q_stage(n):
+            if not ok(n):
+                return
+            w = CHUNKS[n]
+            codes = ring.tile([P, w * P], U32, name="codes", tag="codes%d" % w, align_bytes=64)
+            scl = ring.tile([P, w * P], U8, name="scl", tag="scl%d" % w, align_bytes=64)
+            nc.vector.quantize_mx(out=codes[:].bitcast(FP8X4), scales=scl[:], in_=st["grp", n][:])
+            st["codes", n] = (codes, scl)
+
+        def mx_stage(n):
+            if not ok(n):
+                return
+            w = CHUNKS[n]
+            codes, scl = st["codes", n]
+            for g in range(4):
+                gb = psum.tile([P, w * P], F32, name="gb", tag="bank")
+                wgrp, wc, ws = w_codes[g // 2]
+                cols = slice((g % 2) * P, (g % 2 + 1) * P)
+                nc.tensor.matmul_mx(out=gb[:], lhsT=wc[:, cols].bitcast(FP8X4), lhsT_scale=ws[:, cols],
+                                    rhs=codes[:].bitcast(FP8X4), rhs_scale=scl[:], start=True, stop=True)
+                st["gb", n, g] = gb
+
+        def act_stage(n):
+            if not ok(n):
+                return
+            w = CHUNKS[n]
+            for g in range(4):
+                a = ring.tile([P, w * P], F32, name="gate%d" % g, tag="gate%d_%d" % (g, w))
+                nc.scalar.activation(out=a[:], in_=st["gb", n, g][:], func=(ACT.Tanh if g == 1 else ACT.Sigmoid),
+                                     bias=bias[:, g:g + 1], scale=1.0)
+                st["gate", n, g] = a
+
+        def ot_stage(n):
+            if not ok(n):
+                return
+            w = CHUNKS[n]
+            ob = psum.tile([P, w * P], BF16, name="ob", tag="bank")
+            for j in range(w):
+                g, r = group_of[starts[n] + j]
+                nc.tensor.transpose(out=ob[:, j * P:(j + 1) * P], in_=og[g][:, r * P:(r + 1) * P],
+                                    identity=ident_b[:])
+            st["ob", n] = ob
+
+        def a_stage(n):
+            if not ok(n):
+                return
+            w = CHUNKS[n]
+            a = ring.tile([P, w * P], F32, name="fa", tag="fa%d" % w)
+            nc.vector.tensor_tensor(out=a[:], in0=st["gate", n, 2][:], in1=st["ob", n][:], op=ALU.mult)
+            st["A", n] = a
+
+        def b_stage(n):
+            if not ok(n):
+                return
+            w = CHUNKS[n]
+            b = ring.tile([P, w * P], F32, name="ig", tag="ig%d" % w)
+            nc.gpsimd.tensor_tensor(out=b[:], in0=st["gate", n, 0][:], in1=st["gate", n, 1][:], op=ALU.mult)
+            st["B", n] = b
+
+        def cmode(n):
+            return CMODE[n % len(CMODE)]
+
+        def c_stage(n):
+            if not ok(n) or cmode(n) == "ACC":
+                return
+            w = CHUNKS[n]
+            c = ring.tile([P, w * P], F32, name="cs", tag="cs%d" % w)
+            eng = nc.vector if cmode(n) == "V" else nc.gpsimd
+            eng.tensor_tensor(out=c[:], in0=st["A", n][:], in1=st["B", n][:], op=ALU.add)
+            st["C", n] = c
+
+        def ct_stage(n):
+            if not ok(n):
+                return
+            w = CHUNKS[n]
+            cb = psum.tile([P, w * P], F32, name="cb", tag="bank")
+            for j in range(w):
+                cols = slice(j * P, (j + 1) * P)
+                if cmode(n) == "ACC":
+                    nc.tensor.matmul(out=cb[:, cols], lhsT=st["A", n][:, cols], rhs=ident_f[:],
+                                     is_transpose=True, start=True, stop=False)
+                    nc.tensor.matmul(out=cb[:, cols], lhsT=st["B", n][:, cols], rhs=ident_f[:],
+                                     is_transpose=True, start=False, stop=True)
+                else:
+                    nc.tensor.transpose(out=cb[:, cols], in_=st["C", n][:, cols], identity=ident_f[:])
+            st["cb", n] = cb
+
+        def oot_stage(n):
+            if not ok(n):
+                return
+            w = CHUNKS[n]
+            oo = psum.tile([P, w * P], F32, name="oo", tag="bank")
+            for j in range(w):
+                cols = slice(j * P, (j + 1) * P)
+                nc.tensor.transpose(out=oo[:, cols], in_=st["gate", n, 3][:, cols], identity=ident_f[:])
+            st["oo", n] = oo
+
+        def th_stage(n):
+            if not ok(n):
+                return
+            w = CHUNKS[n]
+            th = ring.tile([P, w * P], F32, name="th", tag="th%d" % w)
+            nc.scalar.activation(out=th[:], in_=st["cb", n][:], func=ACT.Tanh)
+            st["th", n] = th
+
+        def out_stage(n):
+            if not ok(n):
+                return
+            w = CHUNKS[n]
+            cols = slice(starts[n] * H, (starts[n] + w) * H)
+            res_t = res.tile([P, w * H], F32, name="out%d" % n)
+            nc.vector.tensor_tensor(out=res_t[:], in0=st["th", n][:], in1=st["oo", n][:], op=ALU.mult)
+            nc.sync.dma_start(out=out_v[:, cols], in_=res_t[:])
+
+        zt_stage(0)
+        zc_stage(0)
+        zt_stage(1)
+        ot_stage(0)
+        bias_ps = psum.tile([P, P], BF16, name="bias_ps", tag="bank")
+        nc.tensor.transpose(out=bias_ps[:], in_=brow[:], identity=ident_b[:])
+        q_stage(0)
+        nc.vector.tensor_copy(out=bias[:], in_=bias_ps[:, 0:4])
+        zc_stage(1)
+        q_stage(1)
+        for k in range(n_chunks + 2):
+            mx_stage(k)
+            act_stage(k)
+            out_stage(k - 2)
+            zt_stage(k + 2)
+            ot_stage(k + 1)
+            oot_stage(k - 1)
+            b_stage(k)
+            zc_stage(k + 2)
+            a_stage(k)
+            c_stage(k)
+            ct_stage(k - 1)
+            th_stage(k - 1)
+            q_stage(k + 2)

@@ -21,7 +21,7 @@ FLOPS = 2 * BS * IN * 4 * H
 
 CHUNKS = [4] * 16
 LOADS = [4, 4, 8, 16, 16, 16]
-CMODE = ["ACC"]
+CMODE = ["V"]
 
 
 def tile_rnn_unit_t_kernel(tc, input_x, previous_time, previous_layer, old_state,

@@ -19,9 +19,10 @@ IN = XDIM + 2 * H
 NT = BS // P
 FLOPS = 2 * BS * IN * 4 * H
 
-CHUNKS = [4] * 16
-LOADS = [4, 4, 8, 16, 16, 16]
-CMODE = ["V"]
+CHUNKS = [2, 2] + [4] * 14 + [2, 2]
+LOADS = [2, 2, 4, 4, 4, 8, 8, 8, 8, 8, 8]
+OLD_LAG = 2
+CMODE = ["ACC"]
 
 
 def tile_rnn_unit_t_kernel(tc, input_x, previous_time, previous_layer, old_state,
@@ -44,19 +45,20 @@ def tile_rnn_unit_t_kernel(tc, input_x, previous_time, previous_layer, old_state
         psum = ctx.enter_context(tc.psum_pool(name="psum", bufs=8))
         ctx.enter_context(tc.manual_schedule())
 
-        ident_f = const.tile([P, P], F32, name="ident_f")
-        make_identity(nc, ident_f[:])
-        ident_b = const.tile([P, P], BF16, name="ident_b")
-        make_identity(nc, ident_b[:])
         brow = const.tile([P, P], BF16, name="brow")
         nc.vector.memset(brow[:], 0.0)
         warm = const.tile([P, 1], F32, name="warm")
         nc.vector.memset(warm[:], 0.0)
+        nc.scalar.activation(out=warm[:], in_=warm[:], func=ACT.Sigmoid)
+        ident_f = const.tile([P, P], F32, name="ident_f")
+        make_identity(nc, ident_f[:])
 
         group_of = {}
         xg, zg, og = [], [], []
+        bounds = [(sum(LOADS[:g]), sum(LOADS[:g + 1])) for g in range(len(LOADS))]
 
-        def load_group(g, a, b):
+        def load_group(g):
+            a, b = bounds[g]
             n = b - a
             xt = res.tile([P, n * XDIM], BF16, name="x%d" % g)
             nc.sync.dma_start(out=xt[:], in_=x_v[:, a * XDIM:b * XDIM])
@@ -69,30 +71,37 @@ def tile_rnn_unit_t_kernel(tc, input_x, previous_time, previous_layer, old_state
             for t in range(a, b):
                 group_of[t] = (g, t - a)
 
-        def load_old(g, a, b):
+        def load_old(g):
+            a, b = bounds[g]
             ot = res.tile([P, (b - a) * H], BF16, name="old%d" % g)
             nc.sync.dma_start(out=ot[:], in_=old_v[:, a * H:b * H])
             og.append(ot)
 
-        bounds = [(sum(LOADS[:g]), sum(LOADS[:g + 1])) for g in range(len(LOADS))]
-        load_group(0, bounds[0][0], bounds[0][1])
+        def bias_row(eng, g):
+            eng.dma_start(out=brow[g:g + 1, :], in_=b_dram[g].rearrange("(o h) -> o h", o=1))
+
         w_dram = [Wi, Ws, Wf, Wo]
         b_dram = [bi, bs_state, bf, bo]
+        load_group(0)
         w_sb = []
         for g in range(4):
             wt = const.tile([P, IN], BF16, name="w%d" % g)
-            nc.scalar.dma_start(out=wt[:], in_=w_dram[g])
+            nc.sync.dma_start(out=wt[:], in_=w_dram[g])
             w_sb.append(wt)
-        for g in range(4):
-            nc.scalar.dma_start(out=brow[g:g + 1, :], in_=b_dram[g].rearrange("(o h) -> o h", o=1))
-        nc.scalar.activation(out=warm[:], in_=warm[:], func=ACT.Sigmoid)
-        load_old(0, bounds[0][0], bounds[0][1])
-        for g in range(1, len(LOADS)):
-            load_group(g, bounds[g][0], bounds[g][1])
-            load_old(g, bounds[g][0], bounds[g][1])
+        bias_row(nc.sync, 0)
+        for g in range(1, 4):
+            bias_row(nc.gpsimd, g)
+        ident_b = const.tile([P, P], BF16, name="ident_b")
+        make_identity(nc, ident_b[:])
+        for g in range(1, len(LOADS) + OLD_LAG):
+            if g < len(LOADS):
+                load_group(g)
+            if g >= OLD_LAG:
+                load_old(g - OLD_LAG)
 
-        w_codes, w_scales = [], []
-        for h in range(2):
+        w_q = {}
+
+        def wt_stage(h):
             wz = psum.tile([P, 2, 2 * P], F32, name="wz", tag="bank")
             for gg in range(2):
                 words = w_sb[2 * h + gg][:].bitcast(F32)
@@ -102,12 +111,13 @@ def tile_rnn_unit_t_kernel(tc, input_x, previous_time, previous_layer, old_state
             wgrp = const.tile([P, 8 * P], BF16, name="wgrp%d" % h, align_bytes=64)
             nc.scalar.copy(out=wgrp[:].bitcast(F32).rearrange("p (c u) -> p c u", u=2),
                            in_=wz[:].rearrange("p u c -> p c u"))
+            w_q[h] = wgrp
+
+        def wq_stage(h):
             wc = const.tile([P, 2 * P], U32, name="wc%d" % h, align_bytes=64)
             ws = const.tile([P, 2 * P], U8, name="ws%d" % h, align_bytes=64)
-            w_codes.append((wgrp, wc, ws))
-        for h in range(2):
-            wgrp, wc, ws = w_codes[h]
-            nc.vector.quantize_mx(out=wc[:].bitcast(FP8X4), scales=ws[:], in_=wgrp[:])
+            nc.vector.quantize_mx(out=wc[:].bitcast(FP8X4), scales=ws[:], in_=w_q[h][:])
+            w_q[h] = (wc, ws)
 
         bias = const.tile([P, 4], F32, name="bias")
 
@@ -132,7 +142,7 @@ def tile_rnn_unit_t_kernel(tc, input_x, previous_time, previous_layer, old_state
                                             identity=ident_f[:])
                 banks.append((zb, wb))
             st["zb", n] = banks
-            grp = ring.tile([P, w * 4 * P], BF16, name="grp", tag="grp%d" % w, align_bytes=64)
+            grp = ring.tile([P, w * 4 * P], BF16, name="grp", tag="grp", align_bytes=64)
             st["grp", n] = grp
 
         def zc_stage(n):
@@ -149,8 +159,8 @@ def tile_rnn_unit_t_kernel(tc, input_x, previous_time, previous_layer, old_state
             if not ok(n):
                 return
             w = CHUNKS[n]
-            codes = ring.tile([P, w * P], U32, name="codes", tag="codes%d" % w, align_bytes=64)
-            scl = ring.tile([P, w * P], U8, name="scl", tag="scl%d" % w, align_bytes=64)
+            codes = ring.tile([P, w * P], U32, name="codes", tag="codes", align_bytes=64)
+            scl = ring.tile([P, w * P], U8, name="scl", tag="scl", align_bytes=64)
             nc.vector.quantize_mx(out=codes[:].bitcast(FP8X4), scales=scl[:], in_=st["grp", n][:])
             st["codes", n] = (codes, scl)
 
@@ -161,7 +171,7 @@ def tile_rnn_unit_t_kernel(tc, input_x, previous_time, previous_layer, old_state
             codes, scl = st["codes", n]
             for g in range(4):
                 gb = psum.tile([P, w * P], F32, name="gb", tag="bank")
-                wgrp, wc, ws = w_codes[g // 2]
+                wc, ws = w_q[g // 2]
                 cols = slice((g % 2) * P, (g % 2 + 1) * P)
                 nc.tensor.matmul_mx(out=gb[:], lhsT=wc[:, cols].bitcast(FP8X4), lhsT_scale=ws[:, cols],
                                     rhs=codes[:].bitcast(FP8X4), rhs_scale=scl[:], start=True, stop=True)
@@ -172,7 +182,7 @@ def tile_rnn_unit_t_kernel(tc, input_x, previous_time, previous_layer, old_state
                 return
             w = CHUNKS[n]
             for g in range(4):
-                a = ring.tile([P, w * P], F32, name="gate%d" % g, tag="gate%d_%d" % (g, w))
+                a = ring.tile([P, w * P], F32, name="gate%d" % g, tag="gate%d" % g)
                 nc.scalar.activation(out=a[:], in_=st["gb", n, g][:], func=(ACT.Tanh if g == 1 else ACT.Sigmoid),
                                      bias=bias[:, g:g + 1], scale=1.0)
                 st["gate", n, g] = a
@@ -192,7 +202,7 @@ def tile_rnn_unit_t_kernel(tc, input_x, previous_time, previous_layer, old_state
             if not ok(n):
                 return
             w = CHUNKS[n]
-            a = ring.tile([P, w * P], F32, name="fa", tag="fa%d" % w)
+            a = ring.tile([P, w * P], F32, name="fa", tag="fa")
             nc.vector.tensor_tensor(out=a[:], in0=st["gate", n, 2][:], in1=st["ob", n][:], op=ALU.mult)
             st["A", n] = a
 
@@ -200,7 +210,7 @@ def tile_rnn_unit_t_kernel(tc, input_x, previous_time, previous_layer, old_state
             if not ok(n):
                 return
             w = CHUNKS[n]
-            b = ring.tile([P, w * P], F32, name="ig", tag="ig%d" % w)
+            b = ring.tile([P, w * P], F32, name="ig", tag="ig")
             nc.gpsimd.tensor_tensor(out=b[:], in0=st["gate", n, 0][:], in1=st["gate", n, 1][:], op=ALU.mult)
             st["B", n] = b
 
@@ -211,7 +221,7 @@ def tile_rnn_unit_t_kernel(tc, input_x, previous_time, previous_layer, old_state
             if not ok(n) or cmode(n) == "ACC":
                 return
             w = CHUNKS[n]
-            c = ring.tile([P, w * P], F32, name="cs", tag="cs%d" % w)
+            c = ring.tile([P, w * P], F32, name="cs", tag="cs")
             eng = nc.vector if cmode(n) == "V" else nc.gpsimd
             eng.tensor_tensor(out=c[:], in0=st["A", n][:], in1=st["B", n][:], op=ALU.add)
             st["C", n] = c
@@ -246,7 +256,7 @@ def tile_rnn_unit_t_kernel(tc, input_x, previous_time, previous_layer, old_state
             if not ok(n):
                 return
             w = CHUNKS[n]
-            th = ring.tile([P, w * P], F32, name="th", tag="th%d" % w)
+            th = ring.tile([P, w * P], F32, name="th", tag="th")
             nc.scalar.activation(out=th[:], in_=st["cb", n][:], func=ACT.Tanh)
             st["th", n] = th
 
@@ -260,26 +270,29 @@ def tile_rnn_unit_t_kernel(tc, input_x, previous_time, previous_layer, old_state
             nc.sync.dma_start(out=out_v[:, cols], in_=res_t[:])
 
         zt_stage(0)
+        wt_stage(0)
         zc_stage(0)
-        zt_stage(1)
-        ot_stage(0)
+        wt_stage(1)
+        wq_stage(0)
+        q_stage(0)
+        wq_stage(1)
         bias_ps = psum.tile([P, P], BF16, name="bias_ps", tag="bank")
         nc.tensor.transpose(out=bias_ps[:], in_=brow[:], identity=ident_b[:])
-        q_stage(0)
         nc.vector.tensor_copy(out=bias[:], in_=bias_ps[:, 0:4])
+        zt_stage(1)
         zc_stage(1)
-        q_stage(1)
+        ot_stage(0)
         for k in range(n_chunks + 2):
             mx_stage(k)
             act_stage(k)
             out_stage(k - 2)
-            zt_stage(k + 2)
+            q_stage(k + 1)
             ot_stage(k + 1)
             oot_stage(k - 1)
             b_stage(k)
-            zc_stage(k + 2)
             a_stage(k)
             c_stage(k)
             ct_stage(k - 1)
             th_stage(k - 1)
-            q_stage(k + 2)
+            zt_stage(k + 2)
+            zc_stage(k + 2)

@@ -19,10 +19,9 @@ IN = XDIM + 2 * H
 NT = BS // P
 FLOPS = 2 * BS * IN * 4 * H
 
-CHUNKS = [2, 2] + [4] * 14 + [2, 2]
-LOADS = [2, 2, 4, 4, 4, 8, 8, 8, 8, 8, 8]
-OLD_LAG = 2
-CMODE = ["ACC"]
+CHUNKS = [4] * 16
+LOADS = [4, 4, 8, 16, 16, 16]
+CMODE = ["G"]
 
 
 def tile_rnn_unit_t_kernel(tc, input_x, previous_time, previous_layer, old_state,
@@ -45,20 +44,19 @@ def tile_rnn_unit_t_kernel(tc, input_x, previous_time, previous_layer, old_state
         psum = ctx.enter_context(tc.psum_pool(name="psum", bufs=8))
         ctx.enter_context(tc.manual_schedule())
 
+        ident_f = const.tile([P, P], F32, name="ident_f")
+        make_identity(nc, ident_f[:])
+        ident_b = const.tile([P, P], BF16, name="ident_b")
+        make_identity(nc, ident_b[:])
         brow = const.tile([P, P], BF16, name="brow")
         nc.vector.memset(brow[:], 0.0)
         warm = const.tile([P, 1], F32, name="warm")
         nc.vector.memset(warm[:], 0.0)
-        nc.scalar.activation(out=warm[:], in_=warm[:], func=ACT.Sigmoid)
-        ident_f = const.tile([P, P], F32, name="ident_f")
-        make_identity(nc, ident_f[:])
 
         group_of = {}
         xg, zg, og = [], [], []
-        bounds = [(sum(LOADS[:g]), sum(LOADS[:g + 1])) for g in range(len(LOADS))]
 
-        def load_group(g):
-            a, b = bounds[g]
+        def load_group(g, a, b):
             n = b - a
             xt = res.tile([P, n * XDIM], BF16, name="x%d" % g)
             nc.sync.dma_start(out=xt[:], in_=x_v[:, a * XDIM:b * XDIM])
@@ -71,37 +69,30 @@ def tile_rnn_unit_t_kernel(tc, input_x, previous_time, previous_layer, old_state
             for t in range(a, b):
                 group_of[t] = (g, t - a)
 
-        def load_old(g):
-            a, b = bounds[g]
+        def load_old(g, a, b):
             ot = res.tile([P, (b - a) * H], BF16, name="old%d" % g)
             nc.sync.dma_start(out=ot[:], in_=old_v[:, a * H:b * H])
             og.append(ot)
 
-        def bias_row(eng, g):
-            eng.dma_start(out=brow[g:g + 1, :], in_=b_dram[g].rearrange("(o h) -> o h", o=1))
-
+        bounds = [(sum(LOADS[:g]), sum(LOADS[:g + 1])) for g in range(len(LOADS))]
+        load_group(0, bounds[0][0], bounds[0][1])
         w_dram = [Wi, Ws, Wf, Wo]
         b_dram = [bi, bs_state, bf, bo]
-        load_group(0)
         w_sb = []
         for g in range(4):
             wt = const.tile([P, IN], BF16, name="w%d" % g)
-            nc.sync.dma_start(out=wt[:], in_=w_dram[g])
+            nc.scalar.dma_start(out=wt[:], in_=w_dram[g])
             w_sb.append(wt)
-        bias_row(nc.sync, 0)
-        for g in range(1, 4):
-            bias_row(nc.gpsimd, g)
-        ident_b = const.tile([P, P], BF16, name="ident_b")
-        make_identity(nc, ident_b[:])
-        for g in range(1, len(LOADS) + OLD_LAG):
-            if g < len(LOADS):
-                load_group(g)
-            if g >= OLD_LAG:
-                load_old(g - OLD_LAG)
+        for g in range(4):
+            nc.scalar.dma_start(out=brow[g:g + 1, :], in_=b_dram[g].rearrange("(o h) -> o h", o=1))
+        nc.scalar.activation(out=warm[:], in_=warm[:], func=ACT.Sigmoid)
+        load_old(0, bounds[0][0], bounds[0][1])
+        for g in range(1, len(LOADS)):
+            load_group(g, bounds[g][0], bounds[g][1])
+            load_old(g, bounds[g][0], bounds[g][1])
 
-        w_q = {}
-
-        def wt_stage(h):
+        w_codes, w_scales = [], []
+        for h in range(2):
             wz = psum.tile([P, 2, 2 * P], F32, name="wz", tag="bank")
             for gg in range(2):
                 words = w_sb[2 * h + gg][:].bitcast(F32)
@@ -111,13 +102,12 @@ def tile_rnn_unit_t_kernel(tc, input_x, previous_time, previous_layer, old_state
             wgrp = const.tile([P, 8 * P], BF16, name="wgrp%d" % h, align_bytes=64)
             nc.scalar.copy(out=wgrp[:].bitcast(F32).rearrange("p (c u) -> p c u", u=2),
                            in_=wz[:].rearrange("p u c -> p c u"))
-            w_q[h] = wgrp
-
-        def wq_stage(h):
             wc = const.tile([P, 2 * P], U32, name="wc%d" % h, align_bytes=64)
             ws = const.tile([P, 2 * P], U8, name="ws%d" % h, align_bytes=64)
-            nc.vector.quantize_mx(out=wc[:].bitcast(FP8X4), scales=ws[:], in_=w_q[h][:])
-            w_q[h] = (wc, ws)
+            w_codes.append((wgrp, wc, ws))
+        for h in range(2):
+            wgrp, wc, ws = w_codes[h]
+            nc.vector.quantize_mx(out=wc[:].bitcast(FP8X4), scales=ws[:], in_=wgrp[:])
 
         bias = const.tile([P, 4], F32, name="bias")
 
@@ -142,7 +132,7 @@ def tile_rnn_unit_t_kernel(tc, input_x, previous_time, previous_layer, old_state
                                             identity=ident_f[:])
                 banks.append((zb, wb))
             st["zb", n] = banks
-            grp = ring.tile([P, w * 4 * P], BF16, name="grp", tag="grp", align_bytes=64)
+            grp = ring.tile([P, w * 4 * P], BF16, name="grp", tag="grp%d" % w, align_bytes=64)
             st["grp", n] = grp
 
         def zc_stage(n):
@@ -159,8 +149,8 @@ def tile_rnn_unit_t_kernel(tc, input_x, previous_time, previous_layer, old_state
             if not ok(n):
                 return
             w = CHUNKS[n]
-            codes = ring.tile([P, w * P], U32, name="codes", tag="codes", align_bytes=64)
-            scl = ring.tile([P, w * P], U8, name="scl", tag="scl", align_bytes=64)
+            codes = ring.tile([P, w * P], U32, name="codes", tag="codes%d" % w, align_bytes=64)
+            scl = ring.tile([P, w * P], U8, name="scl", tag="scl%d" % w, align_bytes=64)
             nc.vector.quantize_mx(out=codes[:].bitcast(FP8X4), scales=scl[:], in_=st["grp", n][:])
             st["codes", n] = (codes, scl)
 
@@ -171,7 +161,7 @@ def tile_rnn_unit_t_kernel(tc, input_x, previous_time, previous_layer, old_state
             codes, scl = st["codes", n]
             for g in range(4):
                 gb = psum.tile([P, w * P], F32, name="gb", tag="bank")
-                wc, ws = w_q[g // 2]
+                wgrp, wc, ws = w_codes[g // 2]
                 cols = slice((g % 2) * P, (g % 2 + 1) * P)
                 nc.tensor.matmul_mx(out=gb[:], lhsT=wc[:, cols].bitcast(FP8X4), lhsT_scale=ws[:, cols],
                                     rhs=codes[:].bitcast(FP8X4), rhs_scale=scl[:], start=True, stop=True)
@@ -182,7 +172,7 @@ def tile_rnn_unit_t_kernel(tc, input_x, previous_time, previous_layer, old_state
                 return
             w = CHUNKS[n]
             for g in range(4):
-                a = ring.tile([P, w * P], F32, name="gate%d" % g, tag="gate%d" % g)
+                a = ring.tile([P, w * P], F32, name="gate%d" % g, tag="gate%d_%d" % (g, w))
                 nc.scalar.activation(out=a[:], in_=st["gb", n, g][:], func=(ACT.Tanh if g == 1 else ACT.Sigmoid),
                                      bias=bias[:, g:g + 1], scale=1.0)
                 st["gate", n, g] = a
@@ -202,7 +192,7 @@ def tile_rnn_unit_t_kernel(tc, input_x, previous_time, previous_layer, old_state
             if not ok(n):
                 return
             w = CHUNKS[n]
-            a = ring.tile([P, w * P], F32, name="fa", tag="fa")
+            a = ring.tile([P, w * P], F32, name="fa", tag="fa%d" % w)
             nc.vector.tensor_tensor(out=a[:], in0=st["gate", n, 2][:], in1=st["ob", n][:], op=ALU.mult)
             st["A", n] = a
 
@@ -210,7 +200,7 @@ def tile_rnn_unit_t_kernel(tc, input_x, previous_time, previous_layer, old_state
             if not ok(n):
                 return
             w = CHUNKS[n]
-            b = ring.tile([P, w * P], F32, name="ig", tag="ig")
+            b = ring.tile([P, w * P], F32, name="ig", tag="ig%d" % w)
             nc.gpsimd.tensor_tensor(out=b[:], in0=st["gate", n, 0][:], in1=st["gate", n, 1][:], op=ALU.mult)
             st["B", n] = b
 
@@ -221,7 +211,7 @@ def tile_rnn_unit_t_kernel(tc, input_x, previous_time, previous_layer, old_state
             if not ok(n) or cmode(n) == "ACC":
                 return
             w = CHUNKS[n]
-            c = ring.tile([P, w * P], F32, name="cs", tag="cs")
+            c = ring.tile([P, w * P], F32, name="cs", tag="cs%d" % w)
             eng = nc.vector if cmode(n) == "V" else nc.gpsimd
             eng.tensor_tensor(out=c[:], in0=st["A", n][:], in1=st["B", n][:], op=ALU.add)
             st["C", n] = c
@@ -256,7 +246,7 @@ def tile_rnn_unit_t_kernel(tc, input_x, previous_time, previous_layer, old_state
             if not ok(n):
                 return
             w = CHUNKS[n]
-            th = ring.tile([P, w * P], F32, name="th", tag="th")
+            th = ring.tile([P, w * P], F32, name="th", tag="th%d" % w)
             nc.scalar.activation(out=th[:], in_=st["cb", n][:], func=ACT.Tanh)
             st["th", n] = th
 
@@ -270,29 +260,26 @@ def tile_rnn_unit_t_kernel(tc, input_x, previous_time, previous_layer, old_state
             nc.sync.dma_start(out=out_v[:, cols], in_=res_t[:])
 
         zt_stage(0)
-        wt_stage(0)
         zc_stage(0)
-        wt_stage(1)
-        wq_stage(0)
-        q_stage(0)
-        wq_stage(1)
+        zt_stage(1)
+        ot_stage(0)
         bias_ps = psum.tile([P, P], BF16, name="bias_ps", tag="bank")
         nc.tensor.transpose(out=bias_ps[:], in_=brow[:], identity=ident_b[:])
+        q_stage(0)
         nc.vector.tensor_copy(out=bias[:], in_=bias_ps[:, 0:4])
-        zt_stage(1)
         zc_stage(1)
-        ot_stage(0)
+        q_stage(1)
         for k in range(n_chunks + 2):
             mx_stage(k)
             act_stage(k)
             out_stage(k - 2)
-            q_stage(k + 1)
+            zt_stage(k + 2)
             ot_stage(k + 1)
             oot_stage(k - 1)
             b_stage(k)
+            zc_stage(k + 2)
             a_stage(k)
             c_stage(k)
             ct_stage(k - 1)
             th_stage(k - 1)
-            zt_stage(k + 2)
-            zc_stage(k + 2)
+            q_stage(k + 2)

@@ -21,7 +21,7 @@ FLOPS = 2 * BS * IN * 4 * H
 
 CHUNKS = [4] * 16
 LOADS = [4, 4, 8, 16, 16, 16]
-CMODE = ["G"]
+CMODE = ["ACC", "G"]
 
 
 def tile_rnn_unit_t_kernel(tc, input_x, previous_time, previous_layer, old_state,

@@ -20,8 +20,9 @@ NT = BS // P
 FLOPS = 2 * BS * IN * 4 * H
 
 CHUNKS = [4] * 16
-LOADS = [4, 4, 8, 16, 16, 16]
-CMODE = ["ACC", "G"]
+LOADS = [4, 4, 4, 4, 8, 8, 8, 8, 8, 8]
+OLD_LAG = 1
+CMODE = ["G", "ACC"]
 
 
 def tile_rnn_unit_t_kernel(tc, input_x, previous_time, previous_layer, old_state,
@@ -44,19 +45,20 @@ def tile_rnn_unit_t_kernel(tc, input_x, previous_time, previous_layer, old_state
         psum = ctx.enter_context(tc.psum_pool(name="psum", bufs=8))
         ctx.enter_context(tc.manual_schedule())
 
-        ident_f = const.tile([P, P], F32, name="ident_f")
-        make_identity(nc, ident_f[:])
-        ident_b = const.tile([P, P], BF16, name="ident_b")
-        make_identity(nc, ident_b[:])
         brow = const.tile([P, P], BF16, name="brow")
         nc.vector.memset(brow[:], 0.0)
         warm = const.tile([P, 1], F32, name="warm")
         nc.vector.memset(warm[:], 0.0)
+        nc.scalar.activation(out=warm[:], in_=warm[:], func=ACT.Sigmoid)
+        ident_f = const.tile([P, P], F32, name="ident_f")
+        make_identity(nc, ident_f[:])
 
         group_of = {}
         xg, zg, og = [], [], []
+        bounds = [(sum(LOADS[:g]), sum(LOADS[:g + 1])) for g in range(len(LOADS))]
 
-        def load_group(g, a, b):
+        def load_group(g):
+            a, b = bounds[g]
             n = b - a
             xt = res.tile([P, n * XDIM], BF16, name="x%d" % g)
             nc.sync.dma_start(out=xt[:], in_=x_v[:, a * XDIM:b * XDIM])
@@ -69,30 +71,36 @@ def tile_rnn_unit_t_kernel(tc, input_x, previous_time, previous_layer, old_state
             for t in range(a, b):
                 group_of[t] = (g, t - a)
 
-        def load_old(g, a, b):
+        def load_old(g):
+            a, b = bounds[g]
             ot = res.tile([P, (b - a) * H], BF16, name="old%d" % g)
             nc.sync.dma_start(out=ot[:], in_=old_v[:, a * H:b * H])
             og.append(ot)
 
-        bounds = [(sum(LOADS[:g]), sum(LOADS[:g + 1])) for g in range(len(LOADS))]
-        load_group(0, bounds[0][0], bounds[0][1])
+        def bias_row(eng, g):
+            eng.dma_start(out=brow[g:g + 1, :], in_=b_dram[g].rearrange("(o h) -> o h", o=1))
+
         w_dram = [Wi, Ws, Wf, Wo]
         b_dram = [bi, bs_state, bf, bo]
+        load_group(0)
         w_sb = []
         for g in range(4):
             wt = const.tile([P, IN], BF16, name="w%d" % g)
-            nc.scalar.dma_start(out=wt[:], in_=w_dram[g])
+            nc.sync.dma_start(out=wt[:], in_=w_dram[g])
             w_sb.append(wt)
         for g in range(4):
-            nc.scalar.dma_start(out=brow[g:g + 1, :], in_=b_dram[g].rearrange("(o h) -> o h", o=1))
-        nc.scalar.activation(out=warm[:], in_=warm[:], func=ACT.Sigmoid)
-        load_old(0, bounds[0][0], bounds[0][1])
-        for g in range(1, len(LOADS)):
-            load_group(g, bounds[g][0], bounds[g][1])
-            load_old(g, bounds[g][0], bounds[g][1])
+            bias_row(nc.sync, g)
+        ident_b = const.tile([P, P], BF16, name="ident_b")
+        make_identity(nc, ident_b[:])
+        for g in range(1, len(LOADS) + OLD_LAG):
+            if g < len(LOADS):
+                load_group(g)
+            if g >= OLD_LAG:
+                load_old(g - OLD_LAG)
 
-        w_codes, w_scales = [], []
-        for h in range(2):
+        w_q = {}
+
+        def wt_stage(h):
             wz = psum.tile([P, 2, 2 * P], F32, name="wz", tag="bank")
             for gg in range(2):
                 words = w_sb[2 * h + gg][:].bitcast(F32)
@@ -102,12 +110,13 @@ def tile_rnn_unit_t_kernel(tc, input_x, previous_time, previous_layer, old_state
             wgrp = const.tile([P, 8 * P], BF16, name="wgrp%d" % h, align_bytes=64)
             nc.scalar.copy(out=wgrp[:].bitcast(F32).rearrange("p (c u) -> p c u", u=2),
                            in_=wz[:].rearrange("p u c -> p c u"))
+            w_q[h] = wgrp
+
+        def wq_stage(h):
             wc = const.tile([P, 2 * P], U32, name="wc%d" % h, align_bytes=64)
             ws = const.tile([P, 2 * P], U8, name="ws%d" % h, align_bytes=64)
-            w_codes.append((wgrp, wc, ws))
-        for h in range(2):
-            wgrp, wc, ws = w_codes[h]
-            nc.vector.quantize_mx(out=wc[:].bitcast(FP8X4), scales=ws[:], in_=wgrp[:])
+            nc.vector.quantize_mx(out=wc[:].bitcast(FP8X4), scales=ws[:], in_=w_q[h][:])
+            w_q[h] = (wc, ws)
 
         bias = const.tile([P, 4], F32, name="bias")
 
@@ -132,7 +141,7 @@ def tile_rnn_unit_t_kernel(tc, input_x, previous_time, previous_layer, old_state
                                             identity=ident_f[:])
                 banks.append((zb, wb))
             st["zb", n] = banks
-            grp = ring.tile([P, w * 4 * P], BF16, name="grp", tag="grp%d" % w, align_bytes=64)
+            grp = ring.tile([P, w * 4 * P], BF16, name="grp", tag="grp", align_bytes=64)
             st["grp", n] = grp
 
         def zc_stage(n):
@@ -149,8 +158,8 @@ def tile_rnn_unit_t_kernel(tc, input_x, previous_time, previous_layer, old_state
             if not ok(n):
                 return
             w = CHUNKS[n]
-            codes = ring.tile([P, w * P], U32, name="codes", tag="codes%d" % w, align_bytes=64)
-            scl = ring.tile([P, w * P], U8, name="scl", tag="scl%d" % w, align_bytes=64)
+            codes = ring.tile([P, w * P], U32, name="codes", tag="codes", align_bytes=64)
+            scl = ring.tile([P, w * P], U8, name="scl", tag="scl", align_bytes=64)
             nc.vector.quantize_mx(out=codes[:].bitcast(FP8X4), scales=scl[:], in_=st["grp", n][:])
             st["codes", n] = (codes, scl)
 
@@ -161,7 +170,7 @@ def tile_rnn_unit_t_kernel(tc, input_x, previous_time, previous_layer, old_state
             codes, scl = st["codes", n]
             for g in range(4):
                 gb = psum.tile([P, w * P], F32, name="gb", tag="bank")
-                wgrp, wc, ws = w_codes[g // 2]
+                wc, ws = w_q[g // 2]
                 cols = slice((g % 2) * P, (g % 2 + 1) * P)
                 nc.tensor.matmul_mx(out=gb[:], lhsT=wc[:, cols].bitcast(FP8X4), lhsT_scale=ws[:, cols],
                                     rhs=codes[:].bitcast(FP8X4), rhs_scale=scl[:], start=True, stop=True)
@@ -172,7 +181,7 @@ def tile_rnn_unit_t_kernel(tc, input_x, previous_time, previous_layer, old_state
                 return
             w = CHUNKS[n]
             for g in range(4):
-                a = ring.tile([P, w * P], F32, name="gate%d" % g, tag="gate%d_%d" % (g, w))
+                a = ring.tile([P, w * P], F32, name="gate%d" % g, tag="gate%d" % g)
                 nc.scalar.activation(out=a[:], in_=st["gb", n, g][:], func=(ACT.Tanh if g == 1 else ACT.Sigmoid),
                                      bias=bias[:, g:g + 1], scale=1.0)
                 st["gate", n, g] = a
@@ -192,7 +201,7 @@ def tile_rnn_unit_t_kernel(tc, input_x, previous_time, previous_layer, old_state
             if not ok(n):
                 return
             w = CHUNKS[n]
-            a = ring.tile([P, w * P], F32, name="fa", tag="fa%d" % w)
+            a = ring.tile([P, w * P], F32, name="fa", tag="fa")
             nc.vector.tensor_tensor(out=a[:], in0=st["gate", n, 2][:], in1=st["ob", n][:], op=ALU.mult)
             st["A", n] = a
 
@@ -200,7 +209,7 @@ def tile_rnn_unit_t_kernel(tc, input_x, previous_time, previous_layer, old_state
             if not ok(n):
                 return
             w = CHUNKS[n]
-            b = ring.tile([P, w * P], F32, name="ig", tag="ig%d" % w)
+            b = ring.tile([P, w * P], F32, name="ig", tag="ig")
             nc.gpsimd.tensor_tensor(out=b[:], in0=st["gate", n, 0][:], in1=st["gate", n, 1][:], op=ALU.mult)
             st["B", n] = b
 
@@ -211,7 +220,7 @@ def tile_rnn_unit_t_kernel(tc, input_x, previous_time, previous_layer, old_state
             if not ok(n) or cmode(n) == "ACC":
                 return
             w = CHUNKS[n]
-            c = ring.tile([P, w * P], F32, name="cs", tag="cs%d" % w)
+            c = ring.tile([P, w * P], F32, name="cs", tag="cs")
             eng = nc.vector if cmode(n) == "V" else nc.gpsimd
             eng.tensor_tensor(out=c[:], in0=st["A", n][:], in1=st["B", n][:], op=ALU.add)
             st["C", n] = c
@@ -246,7 +255,7 @@ def tile_rnn_unit_t_kernel(tc, input_x, previous_time, previous_layer, old_state
             if not ok(n):
                 return
             w = CHUNKS[n]
-            th = ring.tile([P, w * P], F32, name="th", tag="th%d" % w)
+            th = ring.tile([P, w * P], F32, name="th", tag="th")
             nc.scalar.activation(out=th[:], in_=st["cb", n][:], func=ACT.Tanh)
             st["th", n] = th
 
@@ -260,13 +269,17 @@ def tile_rnn_unit_t_kernel(tc, input_x, previous_time, previous_layer, old_state
             nc.sync.dma_start(out=out_v[:, cols], in_=res_t[:])
 
         zt_stage(0)
+        wt_stage(0)
         zc_stage(0)
+        wt_stage(1)
+        wq_stage(0)
+        q_stage(0)
+        wq_stage(1)
         zt_stage(1)
         ot_stage(0)
         bias_ps = psum.tile([P, P], BF16, name="bias_ps", tag="bank")
         nc.tensor.transpose(out=bias_ps[:], in_=brow[:], identity=ident_b[:])
-        q_stage(0)
-        nc.vector.tensor_copy(out=bias[:], in_=bias_ps[:, 0:4])
+        nc.scalar.copy(out=bias[:], in_=bias_ps[:, 0:4])
         zc_stage(1)
         q_stage(1)
         for k in range(n_chunks + 2):

@@ -89,7 +89,7 @@ def tile_rnn_unit_t_kernel(tc, input_x, previous_time, previous_layer, old_state
             nc.sync.dma_start(out=wt[:], in_=w_dram[g])
             w_sb.append(wt)
         for g in range(4):
-            bias_row(nc.sync, g)
+            bias_row(nc.gpsimd, g)
         ident_b = const.tile([P, P], BF16, name="ident_b")
         make_identity(nc, ident_b[:])
         for g in range(1, len(LOADS) + OLD_LAG):
@@ -130,16 +130,22 @@ def tile_rnn_unit_t_kernel(tc, input_x, previous_time, previous_layer, old_state
                 return
             w = CHUNKS[n]
             banks = []
+            jobs = []
             for h in range((w + 1) // 2):
                 wb = min(2, w - 2 * h)
                 zb = psum.tile([P, 2, wb * P], F32, name="zb", tag="bank")
-                for j in range(wb):
-                    g, r = group_of[starts[n] + 2 * h + j]
-                    for u, src in ((0, xg[g]), (1, zg[g])):
-                        nc.tensor.transpose(out=zb[:, u, j * P:(j + 1) * P],
-                                            in_=src[:].bitcast(F32)[:, r * P:(r + 1) * P],
-                                            identity=ident_f[:])
                 banks.append((zb, wb))
+                for j in range(wb):
+                    for u in range(2):
+                        jobs.append((u, h, j))
+            if n == 0:
+                jobs = sorted(jobs)
+            for u, h, j in jobs:
+                g, r = group_of[starts[n] + 2 * h + j]
+                src = (xg[g], zg[g])[u]
+                nc.tensor.transpose(out=banks[h][0][:, u, j * P:(j + 1) * P],
+                                    in_=src[:].bitcast(F32)[:, r * P:(r + 1) * P],
+                                    identity=ident_f[:])
             st["zb", n] = banks
             grp = ring.tile([P, w * 4 * P], BF16, name="grp", tag="grp", align_bytes=64)
             st["grp", n] = grp
@@ -150,8 +156,11 @@ def tile_rnn_unit_t_kernel(tc, input_x, previous_time, previous_layer, old_state
             gw = st["grp", n][:].bitcast(F32)
             c0 = 0
             for zb, wb in st["zb", n]:
-                nc.vector.tensor_copy(out=gw[:, 2 * c0:2 * (c0 + wb * P)].rearrange("p (c u) -> p c u", u=2),
-                                      in_=zb[:].rearrange("p u c -> p c u"))
+                dst = gw[:, 2 * c0:2 * (c0 + wb * P)].rearrange("p (c u) -> p c u", u=2)
+                if n == 0 and c0 > 0:
+                    nc.scalar.copy(out=dst, in_=zb[:].rearrange("p u c -> p c u"))
+                else:
+                    nc.vector.tensor_copy(out=dst, in_=zb[:].rearrange("p u c -> p c u"))
                 c0 += wb * P
 
         def q_stage(n):
@@ -269,11 +278,11 @@ def tile_rnn_unit_t_kernel(tc, input_x, previous_time, previous_layer, old_state
             nc.sync.dma_start(out=out_v[:, cols], in_=res_t[:])
 
         zt_stage(0)
-        wt_stage(0)
         zc_stage(0)
+        wt_stage(0)
         wt_stage(1)
-        wq_stage(0)
         q_stage(0)
+        wq_stage(0)
         wq_stage(1)
         zt_stage(1)
         ot_stage(0)

@@ -89,7 +89,7 @@ def tile_rnn_unit_t_kernel(tc, input_x, previous_time, previous_layer, old_state
             nc.sync.dma_start(out=wt[:], in_=w_dram[g])
             w_sb.append(wt)
         for g in range(4):
-            bias_row(nc.gpsimd, g)
+            bias_row(nc.sync, g)
         ident_b = const.tile([P, P], BF16, name="ident_b")
         make_identity(nc, ident_b[:])
         for g in range(1, len(LOADS) + OLD_LAG):
@@ -130,22 +130,16 @@ def tile_rnn_unit_t_kernel(tc, input_x, previous_time, previous_layer, old_state
                 return
             w = CHUNKS[n]
             banks = []
-            jobs = []
             for h in range((w + 1) // 2):
                 wb = min(2, w - 2 * h)
                 zb = psum.tile([P, 2, wb * P], F32, name="zb", tag="bank")
-                banks.append((zb, wb))
                 for j in range(wb):
-                    for u in range(2):
-                        jobs.append((u, h, j))
-            if n == 0:
-                jobs = sorted(jobs)
-            for u, h, j in jobs:
-                g, r = group_of[starts[n] + 2 * h + j]
-                src = (xg[g], zg[g])[u]
-                nc.tensor.transpose(out=banks[h][0][:, u, j * P:(j + 1) * P],
-                                    in_=src[:].bitcast(F32)[:, r * P:(r + 1) * P],
-                                    identity=ident_f[:])
+                    g, r = group_of[starts[n] + 2 * h + j]
+                    for u, src in ((0, xg[g]), (1, zg[g])):
+                        nc.tensor.transpose(out=zb[:, u, j * P:(j + 1) * P],
+                                            in_=src[:].bitcast(F32)[:, r * P:(r + 1) * P],
+                                            identity=ident_f[:])
+                banks.append((zb, wb))
             st["zb", n] = banks
             grp = ring.tile([P, w * 4 * P], BF16, name="grp", tag="grp", align_bytes=64)
             st["grp", n] = grp
@@ -156,11 +150,8 @@ def tile_rnn_unit_t_kernel(tc, input_x, previous_time, previous_layer, old_state
             gw = st["grp", n][:].bitcast(F32)
             c0 = 0
             for zb, wb in st["zb", n]:
-                dst = gw[:, 2 * c0:2 * (c0 + wb * P)].rearrange("p (c u) -> p c u", u=2)
-                if n == 0 and c0 > 0:
-                    nc.scalar.copy(out=dst, in_=zb[:].rearrange("p u c -> p c u"))
-                else:
-                    nc.vector.tensor_copy(out=dst, in_=zb[:].rearrange("p u c -> p c u"))
+                nc.vector.tensor_copy(out=gw[:, 2 * c0:2 * (c0 + wb * P)].rearrange("p (c u) -> p c u", u=2),
+                                      in_=zb[:].rearrange("p u c -> p c u"))
                 c0 += wb * P
 
         def q_stage(n):
@@ -278,14 +269,13 @@ def tile_rnn_unit_t_kernel(tc, input_x, previous_time, previous_layer, old_state
             nc.sync.dma_start(out=out_v[:, cols], in_=res_t[:])
 
         zt_stage(0)
-        zc_stage(0)
         wt_stage(0)
+        zc_stage(0)
         wt_stage(1)
-        q_stage(0)
         wq_stage(0)
+        q_stage(0)
         wq_stage(1)
         zt_stage(1)
-        ot_stage(0)
         bias_ps = psum.tile([P, P], BF16, name="bias_ps", tag="bank")
         nc.tensor.transpose(out=bias_ps[:], in_=brow[:], identity=ident_b[:])
         nc.scalar.copy(out=bias[:], in_=bias_ps[:, 0:4])
@@ -296,12 +286,17 @@ def tile_rnn_unit_t_kernel(tc, input_x, previous_time, previous_layer, old_state
             act_stage(k)
             out_stage(k - 2)
             zt_stage(k + 2)
-            ot_stage(k + 1)
-            oot_stage(k - 1)
+            ot_stage(k)
+            if cmode(k - 1) == "ACC":
+                ct_stage(k - 1)
+                oot_stage(k - 1)
+            else:
+                oot_stage(k - 1)
             b_stage(k)
             zc_stage(k + 2)
             a_stage(k)
             c_stage(k)
-            ct_stage(k - 1)
+            if cmode(k - 1) != "ACC":
+                ct_stage(k - 1)
             th_stage(k - 1)
             q_stage(k + 2)

from contextlib import ExitStack

import concourse.bass as bass
import concourse.mybir as mybir
import concourse.tile as tile
from concourse.masks import make_identity

F32 = mybir.dt.float32
BF16 = mybir.dt.bfloat16
U32 = mybir.dt.uint32
U8 = mybir.dt.uint8
FP8X4 = mybir.dt.float8_e4m3fn_x4
ACT = mybir.ActivationFunctionType
ALU = mybir.AluOpType

P = 128
BS, H, XDIM = 8192, 128, 256
IN = XDIM + 2 * H
NT = BS // P
FLOPS = 2 * BS * IN * 4 * H

CHUNKS = [4] * 16
LOADS = [4, 4, 4, 4, 8, 8, 8, 8, 8, 8]
OLD_LAG = 1
CMODE = ["G", "ACC"]


def tile_rnn_unit_t_kernel(tc, input_x, previous_time, previous_layer, old_state,
                                      Wi, bi, Wf, bf, Wo, bo, Ws, bs_state, out):
    nc = tc.nc
    n_chunks = len(CHUNKS)
    starts = [sum(CHUNKS[:n]) for n in range(n_chunks)]
    assert sum(CHUNKS) == NT and sum(LOADS) == NT

    x_v = input_x.rearrange("(p t) k -> p (t k)", t=NT)
    pt_v = previous_time.rearrange("(p t) k -> p t k", t=NT)
    pl_v = previous_layer.rearrange("(p t) k -> p t k", t=NT)
    old_v = old_state.rearrange("(p t) k -> p (t k)", t=NT)
    out_v = out.rearrange("(p t) h -> p (t h)", t=NT)

    with ExitStack() as ctx:
        const = ctx.enter_context(tc.tile_pool(name="const", bufs=1))
        res = ctx.enter_context(tc.tile_pool(name="res", bufs=1))
        ring = ctx.enter_context(tc.tile_pool(name="ring", bufs=4))
        psum = ctx.enter_context(tc.psum_pool(name="psum", bufs=8))
        ctx.enter_context(tc.manual_schedule())

        brow = const.tile([P, P], BF16, name="brow")
        nc.vector.memset(brow[:], 0.0)
        warm = const.tile([P, 1], F32, name="warm")
        nc.vector.memset(warm[:], 0.0)
        nc.scalar.activation(out=warm[:], in_=warm[:], func=ACT.Sigmoid)
        ident_f = const.tile([P, P], F32, name="ident_f")
        make_identity(nc, ident_f[:])

        group_of = {}
        xg, zg, og = [], [], []
        bounds = [(sum(LOADS[:g]), sum(LOADS[:g + 1])) for g in range(len(LOADS))]

        def load_group(g):
            a, b = bounds[g]
            n = b - a
            xt = res.tile([P, n * XDIM], BF16, name="x%d" % g)
            nc.sync.dma_start(out=xt[:], in_=x_v[:, a * XDIM:b * XDIM])
            zt = res.tile([P, n * 2 * H], BF16, name="ptl%d" % g)
            zt4 = zt[:].rearrange("p (t s k) -> p t s k", s=2, k=H)
            nc.sync.dma_start(out=zt4[:, :, 0, :], in_=pt_v[:, a:b, :])
            nc.sync.dma_start(out=zt4[:, :, 1, :], in_=pl_v[:, a:b, :])
            xg.append(xt)
            zg.append(zt)
            for t in range(a, b):
                group_of[t] = (g, t - a)

        def load_old(g):
            a, b = bounds[g]
            ot = res.tile([P, (b - a) * H], BF16, name="old%d" % g)
            nc.sync.dma_start(out=ot[:], in_=old_v[:, a * H:b * H])
            og.append(ot)

        def bias_row(eng, g):
            eng.dma_start(out=brow[g:g + 1, :], in_=b_dram[g].rearrange("(o h) -> o h", o=1))

        w_dram = [Wi, Ws, Wf, Wo]
        b_dram = [bi, bs_state, bf, bo]
        load_group(0)
        w_sb = []
        for g in range(4):
            wt = const.tile([P, IN], BF16, name="w%d" % g)
            nc.sync.dma_start(out=wt[:], in_=w_dram[g])
            w_sb.append(wt)
        for g in range(4):
            bias_row(nc.sync, g)
        ident_b = const.tile([P, P], BF16, name="ident_b")
        make_identity(nc, ident_b[:])
        for g in range(1, len(LOADS) + OLD_LAG):
            if g < len(LOADS):
                load_group(g)
            if g >= OLD_LAG:
                load_old(g - OLD_LAG)

        w_q = {}

        def wt_stage(h):
            wz = psum.tile([P, 2, 2 * P], F32, name="wz", tag="bank")
            for gg in range(2):
                words = w_sb[2 * h + gg][:].bitcast(F32)
                for u in range(2):
                    nc.tensor.transpose(out=wz[:, u, gg * P:(gg + 1) * P], in_=words[:, u * P:(u + 1) * P],
                                        identity=ident_f[:])
            wgrp = const.tile([P, 8 * P], BF16, name="wgrp%d" % h, align_bytes=64)
            nc.scalar.copy(out=wgrp[:].bitcast(F32).rearrange("p (c u) -> p c u", u=2),
                           in_=wz[:].rearrange("p u c -> p c u"))
            w_q[h] = wgrp

        def wq_stage(h):
            wc = const.tile([P, 2 * P], U32, name="wc%d" % h, align_bytes=64)
            ws = const.tile([P, 2 * P], U8, name="ws%d" % h, align_bytes=64)
            nc.vector.quantize_mx(out=wc[:].bitcast(FP8X4), scales=ws[:], in_=w_q[h][:])
            w_q[h] = (wc, ws)

        bias = const.tile([P, 4], F32, name="bias")

        st = {}

        def ok(n):
            return 0 <= n < n_chunks

        def zt_stage(n):
            if not ok(n):
                return
            w = CHUNKS[n]
            banks = []
            for h in range((w + 1) // 2):
                wb = min(2, w - 2 * h)
                zb = psum.tile([P, 2, wb * P], F32, name="zb", tag="bank")
                for j in range(wb):
                    g, r = group_of[starts[n] + 2 * h + j]
                    for u, src in ((0, xg[g]), (1, zg[g])):
                        nc.tensor.transpose(out=zb[:, u, j * P:(j + 1) * P],
                                            in_=src[:].bitcast(F32)[:, r * P:(r + 1) * P],
                                            identity=ident_f[:])
                banks.append((zb, wb))
            st["zb", n] = banks
            grp = ring.tile([P, w * 4 * P], BF16, name="grp", tag="grp", align_bytes=64)
            st["grp", n] = grp

        def zc_stage(n):
            if not ok(n):
                return
            gw = st["grp", n][:].bitcast(F32)
            c0 = 0
            for zb, wb in st["zb", n]:
                nc.vector.tensor_copy(out=gw[:, 2 * c0:2 * (c0 + wb * P)].rearrange("p (c u) -> p c u", u=2),
                                      in_=zb[:].rearrange("p u c -> p c u"))
                c0 += wb * P

        def q_stage(n):
            if not ok(n):
                return
            w = CHUNKS[n]
            codes = ring.tile([P, w * P], U32, name="codes", tag="codes", align_bytes=64)
            scl = ring.tile([P, w * P], U8, name="scl", tag="scl", align_bytes=64)
            nc.vector.quantize_mx(out=codes[:].bitcast(FP8X4), scales=scl[:], in_=st["grp", n][:])
            st["codes", n] = (codes, scl)

        def mx_stage(n):
            if not ok(n):
                return
            w = CHUNKS[n]
            codes, scl = st["codes", n]
            for g in range(4):
                gb = psum.tile([P, w * P], F32, name="gb", tag="bank")
                wc, ws = w_q[g // 2]
                cols = slice((g % 2) * P, (g % 2 + 1) * P)
                nc.tensor.matmul_mx(out=gb[:], lhsT=wc[:, cols].bitcast(FP8X4), lhsT_scale=ws[:, cols],
                                    rhs=codes[:].bitcast(FP8X4), rhs_scale=scl[:], start=True, stop=True)
                st["gb", n, g] = gb

        def act_stage(n):
            if not ok(n):
                return
            w = CHUNKS[n]
            for g in range(4):
                a = ring.tile([P, w * P], F32, name="gate%d" % g, tag="gate%d" % g)
                nc.scalar.activation(out=a[:], in_=st["gb", n, g][:], func=(ACT.Tanh if g == 1 else ACT.Sigmoid),
                                     bias=bias[:, g:g + 1], scale=1.0)
                st["gate", n, g] = a

        def ot_stage(n):
            if not ok(n):
                return
            w = CHUNKS[n]
            ob = psum.tile([P, w * P], BF16, name="ob", tag="bank")
            for j in range(w):
                g, r = group_of[starts[n] + j]
                nc.tensor.transpose(out=ob[:, j * P:(j + 1) * P], in_=og[g][:, r * P:(r + 1) * P],
                                    identity=ident_b[:])
            st["ob", n] = ob

        def a_stage(n):
            if not ok(n):
                return
            w = CHUNKS[n]
            a = ring.tile([P, w * P], F32, name="fa", tag="fa")
            nc.vector.tensor_tensor(out=a[:], in0=st["gate", n, 2][:], in1=st["ob", n][:], op=ALU.mult)
            st["A", n] = a

        def b_stage(n):
            if not ok(n):
                return
            w = CHUNKS[n]
            b = ring.tile([P, w * P], F32, name="ig", tag="ig")
            nc.gpsimd.tensor_tensor(out=b[:], in0=st["gate", n, 0][:], in1=st["gate", n, 1][:], op=ALU.mult)
            st["B", n] = b

        def cmode(n):
            return CMODE[n % len(CMODE)]

        def c_stage(n):
            if not ok(n) or cmode(n) == "ACC":
                return
            w = CHUNKS[n]
            c = ring.tile([P, w * P], F32, name="cs", tag="cs")
            eng = nc.vector if cmode(n) == "V" else nc.gpsimd
            eng.tensor_tensor(out=c[:], in0=st["A", n][:], in1=st["B", n][:], op=ALU.add)
            st["C", n] = c

        def ct_stage(n):
            if not ok(n):
                return
            w = CHUNKS[n]
            cb = psum.tile([P, w * P], F32, name="cb", tag="bank")
            for j in range(w):
                cols = slice(j * P, (j + 1) * P)
                if cmode(n) == "ACC":
                    nc.tensor.matmul(out=cb[:, cols], lhsT=st["A", n][:, cols], rhs=ident_f[:],
                                     is_transpose=True, start=True, stop=False)
                    nc.tensor.matmul(out=cb[:, cols], lhsT=st["B", n][:, cols], rhs=ident_f[:],
                                     is_transpose=True, start=False, stop=True)
                else:
                    nc.tensor.transpose(out=cb[:, cols], in_=st["C", n][:, cols], identity=ident_f[:])
            st["cb", n] = cb

        def oot_stage(n):
            if not ok(n):
                return
            w = CHUNKS[n]
            oo = psum.tile([P, w * P], F32, name="oo", tag="bank")
            for j in range(w):
                cols = slice(j * P, (j + 1) * P)
                nc.tensor.transpose(out=oo[:, cols], in_=st["gate", n, 3][:, cols], identity=ident_f[:])
            st["oo", n] = oo

        def th_stage(n):
            if not ok(n):
                return
            w = CHUNKS[n]
            th = ring.tile([P, w * P], F32, name="th", tag="th")
            nc.scalar.activation(out=th[:], in_=st["cb", n][:], func=ACT.Tanh)
            st["th", n] = th

        def out_stage(n):
            if not ok(n):
                return
            w = CHUNKS[n]
            cols = slice(starts[n] * H, (starts[n] + w) * H)
            res_t = res.tile([P, w * H], F32, name="out%d" % n)
            nc.vector.tensor_tensor(out=res_t[:], in0=st["th", n][:], in1=st["oo", n][:], op=ALU.mult)
            nc.sync.dma_start(out=out_v[:, cols], in_=res_t[:])

        zt_stage(0)
        wt_stage(0)
        zc_stage(0)
        wt_stage(1)
        wq_stage(0)
        q_stage(0)
        wq_stage(1)
        zt_stage(1)
        bias_ps = psum.tile([P, P], BF16, name="bias_ps", tag="bank")
        nc.tensor.transpose(out=bias_ps[:], in_=brow[:], identity=ident_b[:])
        nc.scalar.copy(out=bias[:], in_=bias_ps[:, 0:4])
        zc_stage(1)
        q_stage(1)
        for k in range(n_chunks + 2):
            mx_stage(k)
            act_stage(k)
            out_stage(k - 2)
            zt_stage(k + 2)
            ot_stage(k)
            if cmode(k - 1) == "ACC":
                ct_stage(k - 1)
                oot_stage(k - 1)
            else:
                oot_stage(k - 1)
            b_stage(k)
            zc_stage(k + 2)
            a_stage(k)
            c_stage(k)
            if cmode(k - 1) != "ACC":
                ct_stage(k - 1)
            th_stage(k - 1)
            q_stage(k + 2)
